import numpy as np
import ml_dtypes

BF16 = ml_dtypes.bfloat16


def bf(x):
    return np.asarray(x, np.float32).astype(BF16)


def f32(x):
    return np.asarray(x, np.float32)


def f64(x):
    return np.asarray(x).astype(np.float64)


def striped(idx):
    return np.tile(idx.reshape(-1, 16).T, (8, 1))


B, S, T, K, E, N = 256, 256, 128, 3, 8, 384


def setup_inputs():
    return {"x": f32(np.random.random((B, S))), "cpds": f32(0.5 * np.random.standard_normal((E, T))), "offs": striped(np.random.permutation(np.tile(np.arange(S), 2))[:N])}


def reference(x, cpds, offs):
    idx = offs[:16].T.reshape(-1)
    v = f64(x)[:, idx].reshape(B, K, T)
    p = np.ones((B, E, T))
    for i in range(K):
        bit = f64((np.arange(E) >> (K - 1 - i)) & 1)[None, :, None]
        vi = v[:, i:i + 1, :]
        p = p * (bit * vi + (1.0 - bit) * (1.0 - vi))
    return (p * f64(cpds)[None, :, :]).sum(axis=(1, 2))[:, None]

@@ -1,0 +1,72 @@
+import concourse.mybir as mybir
+from concourse.masks import make_identity
+
+F32 = mybir.dt.float32
+U16 = mybir.dt.uint16
+MULT = mybir.AluOpType.mult
+ADD = mybir.AluOpType.add
+SUBTRACT = mybir.AluOpType.subtract
+
+P = 128
+B, S = 256, 256
+T, K, E = 128, 3, 8
+N = K * T
+BLOCKS = B // P
+LIST_COLS = T // 16
+
+
+def bit_halves(rows, low):
+    view = rows.rearrange("p (h two l) -> p h two l", two=2, l=low)
+    return view[:, :, 0, :], view[:, :, 1, :]
+
+
+def tile_binarybnmodel_kernel(tc, x, cpds, offs, out):
+    nc = tc.nc
+    with (
+        tc.tile_pool(name="held", bufs=1) as held,
+        tc.tile_pool(name="work", bufs=2) as work,
+        tc.psum_pool(name="psum", bufs=1) as psum,
+    ):
+        offsets = held.tile([P, N // 16], U16, name="offsets")
+        nc.sync.dma_start(offsets[:], offs)
+
+        coef = held.tile([P, E * T], F32, name="coef")
+        nc.gpsimd.dma_start(coef[:], cpds.rearrange("e t -> (e t)").partition_broadcast(P))
+
+        windows = []
+        for blk in range(BLOCKS):
+            window = held.tile([P, S], F32, name=f"window{blk}")
+            nc.scalar.dma_start(window[:], x[blk * P : (blk + 1) * P, :])
+            windows.append(window)
+
+        identity = held.tile([P, P], F32, name="identity")
+        make_identity(nc, identity[:])
+
+        for low in (T, 2 * T, 4 * T):
+            bit_clear, bit_set = bit_halves(coef[:], low)
+            nc.vector.tensor_tensor(bit_set, bit_set, bit_clear, SUBTRACT)
+
+        sums = held.tile([P, BLOCKS], F32, name="sums")
+        for blk in range(BLOCKS):
+            level = coef
+            for i in reversed(range(K)):
+                rows = 2**i
+                folded = work.tile([P, rows * T], F32, name=f"folded{i}")
+                for m in range(rows):
+                    nc.vector.tensor_tensor(
+                        folded[:, m * T : (m + 1) * T],
+                        windows[blk][:].indirect(offsets[:, i * LIST_COLS : (i + 1) * LIST_COLS]),
+                        level[:, (2 * m + 1) * T : (2 * m + 2) * T],
+                        MULT,
+                    )
+                without_v, _ = bit_halves(level[:], T)
+                folded_rows = folded[:].rearrange("p (m t) -> p m t", t=T)
+                nc.vector.tensor_tensor(folded_rows, folded_rows, without_v, ADD)
+                level = folded
+            nc.vector.tensor_reduce(sums[:, blk : blk + 1], level[:], mybir.AxisListType.X, ADD)
+
+        sums_t_psum = psum.tile([BLOCKS, P], F32, name="sums_t_psum")
+        nc.tensor.transpose(sums_t_psum[:], sums[:], identity[:])
+        sums_t = held.tile([BLOCKS, P], F32, name="sums_t")
+        nc.vector.tensor_copy(sums_t[:], sums_t_psum[:])
+        nc.sync.dma_start(out.rearrange("(n p) o -> n (p o)", p=P), sums_t[:])

@@ -6,6 +6,7 @@ U16 = mybir.dt.uint16
 MULT = mybir.AluOpType.mult
 ADD = mybir.AluOpType.add
 SUBTRACT = mybir.AluOpType.subtract
+COPY = mybir.ActivationFunctionType.Copy
 
 P = 128
 B, S = 256, 256
@@ -24,19 +25,18 @@ def tile_binarybnmodel_kernel(tc, x, cpds, offs, out):
     nc = tc.nc
     with (
         tc.tile_pool(name="held", bufs=1) as held,
-        tc.tile_pool(name="work", bufs=2) as work,
         tc.psum_pool(name="psum", bufs=1) as psum,
     ):
         offsets = held.tile([P, N // 16], U16, name="offsets")
         nc.sync.dma_start(offsets[:], offs)
 
         coef = held.tile([P, E * T], F32, name="coef")
-        nc.gpsimd.dma_start(coef[:], cpds.rearrange("e t -> (e t)").partition_broadcast(P))
+        nc.scalar.dma_start(coef[:], cpds.rearrange("e t -> (e t)").partition_broadcast(P))
 
         windows = []
         for blk in range(BLOCKS):
             window = held.tile([P, S], F32, name=f"window{blk}")
-            nc.scalar.dma_start(window[:], x[blk * P : (blk + 1) * P, :])
+            nc.sync.dma_start(window[:], x[blk * P : (blk + 1) * P, :])
             windows.append(window)
 
         identity = held.tile([P, P], F32, name="identity")
@@ -46,27 +46,37 @@ def tile_binarybnmodel_kernel(tc, x, cpds, offs, out):
             bit_clear, bit_set = bit_halves(coef[:], low)
             nc.vector.tensor_tensor(bit_set, bit_set, bit_clear, SUBTRACT)
 
-        sums = held.tile([P, BLOCKS], F32, name="sums")
-        for blk in range(BLOCKS):
-            level = coef
-            for i in reversed(range(K)):
-                rows = 2**i
-                folded = work.tile([P, rows * T], F32, name=f"folded{i}")
-                for m in range(rows):
+        summed = held.tile([P, K * T], F32, name="summed")
+        constant = held.tile([P, 1], F32, name="constant")
+        nc.scalar.activation(summed[:, 0:T], coef[:, 0:T], COPY, accum_out=constant[:])
+
+        terms = [held.tile([P, K * T], F32, name=f"terms{blk}") for blk in range(BLOCKS)]
+        levels = [coef for blk in range(BLOCKS)]
+        for i in reversed(range(K)):
+            rows = 2**i
+            folded = [held.tile([P, rows * T], F32, name=f"folded{i}_{blk}") for blk in range(BLOCKS)]
+            for m in reversed(range(rows)):
+                for blk in range(BLOCKS):
+                    product = terms[blk][:, i * T : (i + 1) * T] if m == 0 else folded[blk][:, m * T : (m + 1) * T]
                     nc.vector.tensor_tensor(
-                        folded[:, m * T : (m + 1) * T],
+                        product,
                         windows[blk][:].indirect(offsets[:, i * LIST_COLS : (i + 1) * LIST_COLS]),
-                        level[:, (2 * m + 1) * T : (2 * m + 2) * T],
+                        levels[blk][:, (2 * m + 1) * T : (2 * m + 2) * T],
                         MULT,
                     )
-                without_v, _ = bit_halves(level[:], T)
-                folded_rows = folded[:].rearrange("p (m t) -> p m t", t=T)
-                nc.vector.tensor_tensor(folded_rows, folded_rows, without_v, ADD)
-                level = folded
-            nc.vector.tensor_reduce(sums[:, blk : blk + 1], level[:], mybir.AxisListType.X, ADD)
+            if rows > 1:
+                for blk in range(BLOCKS):
+                    without_v = bit_halves(levels[blk][:], T)[0][:, 1:, :]
+                    products = folded[blk][:, T:].rearrange("p (m t) -> p m t", t=T)
+                    nc.vector.tensor_tensor(products, products, without_v, ADD)
+            levels = folded
+
+        sums = held.tile([P, BLOCKS], F32, name="sums")
+        for blk in range(BLOCKS):
+            nc.scalar.activation(summed[:], terms[blk][:], COPY, accum_out=sums[:, blk : blk + 1])
 
         sums_t_psum = psum.tile([BLOCKS, P], F32, name="sums_t_psum")
         nc.tensor.transpose(sums_t_psum[:], sums[:], identity[:])
         sums_t = held.tile([BLOCKS, P], F32, name="sums_t")
-        nc.vector.tensor_copy(sums_t[:], sums_t_psum[:])
+        nc.vector.tensor_scalar(sums_t[:], sums_t_psum[:], constant[0:BLOCKS, :], None, ADD)
         nc.sync.dma_start(out.rearrange("(n p) o -> n (p o)", p=P), sums_t[:])

@@ -26,12 +26,13 @@ def tile_binarybnmodel_kernel(tc, x, cpds, offs, out):
     with (
         tc.tile_pool(name="held", bufs=1) as held,
         tc.psum_pool(name="psum", bufs=1) as psum,
+        tc.psum_pool(name="rows_psum", bufs=4) as rows_psum,
     ):
         offsets = held.tile([P, N // 16], U16, name="offsets")
         nc.sync.dma_start(offsets[:], offs)
 
-        coef = held.tile([P, E * T], F32, name="coef")
-        nc.scalar.dma_start(coef[:], cpds.rearrange("e t -> (e t)").partition_broadcast(P))
+        entries = held.tile([E, T], F32, name="entries")
+        nc.scalar.dma_start(entries[:], cpds)
 
         windows = []
         for blk in range(BLOCKS):
@@ -39,16 +40,29 @@ def tile_binarybnmodel_kernel(tc, x, cpds, offs, out):
             nc.sync.dma_start(window[:], x[blk * P : (blk + 1) * P, :])
             windows.append(window)
 
+        weights = held.tile([E, E], F32, name="weights")
+        make_identity(nc, weights[:])
+        for low in (1, 2, 4):
+            bit_clear, bit_set = bit_halves(weights[:], low)
+            nc.vector.tensor_tensor(bit_set, bit_set, bit_clear, SUBTRACT)
+        spread = held.tile([E, E * P], F32, name="spread")
+        nc.vector.tensor_copy(
+            spread[:].rearrange("e (s b) -> e s b", b=P), weights[:].unsqueeze(2).to_broadcast([E, E, P])
+        )
+
         identity = held.tile([P, P], F32, name="identity")
         make_identity(nc, identity[:])
 
-        for low in (T, 2 * T, 4 * T):
-            bit_clear, bit_set = bit_halves(coef[:], low)
-            nc.vector.tensor_tensor(bit_set, bit_set, bit_clear, SUBTRACT)
-
+        coef = held.tile([P, E * T], F32, name="coef")
         summed = held.tile([P, K * T], F32, name="summed")
         constant = held.tile([P, 1], F32, name="constant")
-        nc.scalar.activation(summed[:, 0:T], coef[:, 0:T], COPY, accum_out=constant[:])
+        for s in list(range(E - 1, 0, -2)) + list(range(E - 2, -1, -2)):
+            coef_psum = rows_psum.tile([P, T], F32, name="coef_psum")
+            nc.tensor.matmul(coef_psum[:], spread[:, s * P : (s + 1) * P], entries[:], start=True, stop=True)
+            if s > 0:
+                nc.scalar.copy(coef[:, s * T : (s + 1) * T], coef_psum[:])
+            else:
+                nc.scalar.activation(summed[:, 0:T], coef_psum[:], COPY, accum_out=constant[:])
 
         terms = [held.tile([P, K * T], F32, name=f"terms{blk}") for blk in range(BLOCKS)]
         levels = [coef for blk in range(BLOCKS)]

@@ -14,6 +14,7 @@ T, K, E = 128, 3, 8
 N = K * T
 BLOCKS = B // P
 LIST_COLS = T // 16
+SQUARE = 32
 
 
 def bit_halves(rows, low):
@@ -25,7 +26,6 @@ def tile_binarybnmodel_kernel(tc, x, cpds, offs, out):
     nc = tc.nc
     with (
         tc.tile_pool(name="held", bufs=1) as held,
-        tc.psum_pool(name="psum", bufs=1) as psum,
         tc.psum_pool(name="rows_psum", bufs=4) as rows_psum,
     ):
         offsets = held.tile([P, N // 16], U16, name="offsets")
@@ -45,20 +45,14 @@ def tile_binarybnmodel_kernel(tc, x, cpds, offs, out):
         for low in (1, 2, 4):
             bit_clear, bit_set = bit_halves(weights[:], low)
             nc.vector.tensor_tensor(bit_set, bit_set, bit_clear, SUBTRACT)
-        spread = held.tile([E, E * P], F32, name="spread")
-        nc.vector.tensor_copy(
-            spread[:].rearrange("e (s b) -> e s b", b=P), weights[:].unsqueeze(2).to_broadcast([E, E, P])
-        )
-
-        identity = held.tile([P, P], F32, name="identity")
-        make_identity(nc, identity[:])
 
         coef = held.tile([P, E * T], F32, name="coef")
         summed = held.tile([P, K * T], F32, name="summed")
         constant = held.tile([P, 1], F32, name="constant")
         for s in list(range(E - 1, 0, -2)) + list(range(E - 2, -1, -2)):
             coef_psum = rows_psum.tile([P, T], F32, name="coef_psum")
-            nc.tensor.matmul(coef_psum[:], spread[:, s * P : (s + 1) * P], entries[:], start=True, stop=True)
+            to_all_partitions = weights[:, s : s + 1].to_broadcast([E, P])
+            nc.tensor.matmul(coef_psum[:], to_all_partitions, entries[:], start=True, stop=True)
             if s > 0:
                 nc.scalar.copy(coef[:, s * T : (s + 1) * T], coef_psum[:])
             else:
@@ -85,12 +79,14 @@ def tile_binarybnmodel_kernel(tc, x, cpds, offs, out):
                     nc.vector.tensor_tensor(products, products, without_v, ADD)
             levels = folded
 
-        sums = held.tile([P, BLOCKS], F32, name="sums")
+        sums = held.tile([P, SQUARE], F32, name="sums", align_bytes=64)
+        nc.gpsimd.memset(sums[:], 0.0)
         for blk in range(BLOCKS):
             nc.scalar.activation(summed[:], terms[blk][:], COPY, accum_out=sums[:, blk : blk + 1])
 
-        sums_t_psum = psum.tile([BLOCKS, P], F32, name="sums_t_psum")
-        nc.tensor.transpose(sums_t_psum[:], sums[:], identity[:])
-        sums_t = held.tile([BLOCKS, P], F32, name="sums_t")
-        nc.vector.tensor_scalar(sums_t[:], sums_t_psum[:], constant[0:BLOCKS, :], None, ADD)
-        nc.sync.dma_start(out.rearrange("(n p) o -> n (p o)", p=P), sums_t[:])
+        sums_t = held.tile([P, SQUARE], F32, name="sums_t", align_bytes=64)
+        nc.vector.transpose(sums_t[:], sums[:])
+        nc.vector.tensor_scalar(sums_t[:], sums_t[:], constant[:], None, ADD)
+        runs = sums_t[:].rearrange("(q j) i -> j q i", j=SQUARE)
+        for blk, queue in zip(range(BLOCKS), (nc.sync, nc.scalar)):
+            queue.dma_start(out[blk * P : (blk + 1) * P, :].rearrange("(q i) o -> q (i o)", i=SQUARE), runs[blk])

@@ -26,7 +26,7 @@ def tile_binarybnmodel_kernel(tc, x, cpds, offs, out):
     nc = tc.nc
     with (
         tc.tile_pool(name="held", bufs=1) as held,
-        tc.psum_pool(name="rows_psum", bufs=4) as rows_psum,
+        tc.psum_pool(name="psum", bufs=4) as psum,
     ):
         offsets = held.tile([P, N // 16], U16, name="offsets")
         nc.sync.dma_start(offsets[:], offs)
@@ -46,47 +46,60 @@ def tile_binarybnmodel_kernel(tc, x, cpds, offs, out):
             bit_clear, bit_set = bit_halves(weights[:], low)
             nc.vector.tensor_tensor(bit_set, bit_set, bit_clear, SUBTRACT)
 
+        early = [held.tile([P, K * T], F32, name=f"early{blk}") for blk in range(BLOCKS)]
+        late = held.tile([P, BLOCKS * T], F32, name="late")
+
         coef = held.tile([P, E * T], F32, name="coef")
-        summed = held.tile([P, K * T], F32, name="summed")
-        constant = held.tile([P, 1], F32, name="constant")
         for s in list(range(E - 1, 0, -2)) + list(range(E - 2, -1, -2)):
-            coef_psum = rows_psum.tile([P, T], F32, name="coef_psum")
+            coef_psum = psum.tile([P, T], F32, name="coef_psum")
             to_all_partitions = weights[:, s : s + 1].to_broadcast([E, P])
             nc.tensor.matmul(coef_psum[:], to_all_partitions, entries[:], start=True, stop=True)
             if s > 0:
                 nc.scalar.copy(coef[:, s * T : (s + 1) * T], coef_psum[:])
             else:
-                nc.scalar.activation(summed[:, 0:T], coef_psum[:], COPY, accum_out=constant[:])
+                for blk in range(BLOCKS):
+                    nc.scalar.copy(early[blk][:, 0:T], coef_psum[:])
 
-        terms = [held.tile([P, K * T], F32, name=f"terms{blk}") for blk in range(BLOCKS)]
         levels = [coef for blk in range(BLOCKS)]
         for i in reversed(range(K)):
             rows = 2**i
-            folded = [held.tile([P, rows * T], F32, name=f"folded{i}_{blk}") for blk in range(BLOCKS)]
+            picked = [
+                windows[blk][:].indirect(offsets[:, i * LIST_COLS : (i + 1) * LIST_COLS]) for blk in range(BLOCKS)
+            ]
+            if rows > 1:
+                folded = [held.tile([P, rows * T], F32, name=f"folded{i}_{blk}") for blk in range(BLOCKS)]
             for m in reversed(range(rows)):
                 for blk in range(BLOCKS):
-                    product = terms[blk][:, i * T : (i + 1) * T] if m == 0 else folded[blk][:, m * T : (m + 1) * T]
-                    nc.vector.tensor_tensor(
-                        product,
-                        windows[blk][:].indirect(offsets[:, i * LIST_COLS : (i + 1) * LIST_COLS]),
-                        levels[blk][:, (2 * m + 1) * T : (2 * m + 2) * T],
-                        MULT,
-                    )
+                    if m > 0:
+                        product = folded[blk][:, m * T : (m + 1) * T]
+                    elif i > 0:
+                        product = early[blk][:, i * T : (i + 1) * T]
+                    else:
+                        product = late[:, blk * T : (blk + 1) * T]
+                    with_v = levels[blk][:, (2 * m + 1) * T : (2 * m + 2) * T]
+                    nc.vector.tensor_tensor(product, picked[blk], with_v, MULT)
             if rows > 1:
                 for blk in range(BLOCKS):
                     without_v = bit_halves(levels[blk][:], T)[0][:, 1:, :]
                     products = folded[blk][:, T:].rearrange("p (m t) -> p m t", t=T)
                     nc.vector.tensor_tensor(products, products, without_v, ADD)
-            levels = folded
+                levels = folded
+
+        early_sums = held.tile([P, BLOCKS], F32, name="early_sums")
+        unused = held.tile([P, K * T], F32, name="unused")
+        for blk in range(BLOCKS):
+            nc.scalar.activation(unused[:], early[blk][:], COPY, accum_out=early_sums[:, blk : blk + 1])
+        late_sums = held.tile([P, BLOCKS], F32, name="late_sums")
+        nc.vector.tensor_reduce(
+            late_sums[:], late[:].rearrange("p (n t) -> p n t", t=T), mybir.AxisListType.X, ADD
+        )
 
         sums = held.tile([P, SQUARE], F32, name="sums", align_bytes=64)
         nc.gpsimd.memset(sums[:], 0.0)
-        for blk in range(BLOCKS):
-            nc.scalar.activation(summed[:], terms[blk][:], COPY, accum_out=sums[:, blk : blk + 1])
+        nc.vector.tensor_tensor(sums[:, 0:BLOCKS], late_sums[:], early_sums[:], ADD)
 
         sums_t = held.tile([P, SQUARE], F32, name="sums_t", align_bytes=64)
         nc.vector.transpose(sums_t[:], sums[:])
-        nc.vector.tensor_scalar(sums_t[:], sums_t[:], constant[:], None, ADD)
         runs = sums_t[:].rearrange("(q j) i -> j q i", j=SQUARE)
         for blk, queue in zip(range(BLOCKS), (nc.sync, nc.scalar)):
             queue.dma_start(out[blk * P : (blk + 1) * P, :].rearrange("(q i) o -> q (i o)", i=SQUARE), runs[blk])

@@ -6,7 +6,7 @@ U16 = mybir.dt.uint16
 MULT = mybir.AluOpType.mult
 ADD = mybir.AluOpType.add
 SUBTRACT = mybir.AluOpType.subtract
-COPY = mybir.ActivationFunctionType.Copy
+IDENTITY = mybir.ActivationFunctionType.Identity
 
 P = 128
 B, S = 256, 256
@@ -14,7 +14,6 @@ T, K, E = 128, 3, 8
 N = K * T
 BLOCKS = B // P
 LIST_COLS = T // 16
-SQUARE = 32
 
 
 def bit_halves(rows, low):
@@ -26,7 +25,7 @@ def tile_binarybnmodel_kernel(tc, x, cpds, offs, out):
     nc = tc.nc
     with (
         tc.tile_pool(name="held", bufs=1) as held,
-        tc.psum_pool(name="psum", bufs=4) as psum,
+        tc.psum_pool(name="psum", bufs=1) as psum,
     ):
         offsets = held.tile([P, N // 16], U16, name="offsets")
         nc.sync.dma_start(offsets[:], offs)
@@ -45,61 +44,54 @@ def tile_binarybnmodel_kernel(tc, x, cpds, offs, out):
         for low in (1, 2, 4):
             bit_clear, bit_set = bit_halves(weights[:], low)
             nc.vector.tensor_tensor(bit_set, bit_set, bit_clear, SUBTRACT)
+            nc.vector.tensor_tensor(bit_clear, bit_clear, bit_set, ADD)
 
-        early = [held.tile([P, K * T], F32, name=f"early{blk}") for blk in range(BLOCKS)]
-        late = held.tile([P, BLOCKS * T], F32, name="late")
+        coef_psum = psum.tile([T, E], F32, name="coef_psum")
+        nc.tensor.matmul(coef_psum[:], entries[:], weights[:], start=True, stop=True)
+        coef = held.tile([T, E], F32, name="coef")
+        nc.scalar.activation(coef[:], coef_psum[:], IDENTITY)
 
-        coef = held.tile([P, E * T], F32, name="coef")
-        for s in list(range(E - 1, 0, -2)) + list(range(E - 2, -1, -2)):
-            coef_psum = psum.tile([P, T], F32, name="coef_psum")
-            to_all_partitions = weights[:, s : s + 1].to_broadcast([E, P])
-            nc.tensor.matmul(coef_psum[:], to_all_partitions, entries[:], start=True, stop=True)
-            if s > 0:
-                nc.scalar.copy(coef[:, s * T : (s + 1) * T], coef_psum[:])
-            else:
-                for blk in range(BLOCKS):
-                    nc.scalar.copy(early[blk][:, 0:T], coef_psum[:])
+        def d(s):
+            return coef[:, s : s + 1]
 
-        levels = [coef for blk in range(BLOCKS)]
+        identity = held.tile([P, P], F32, name="identity")
+        make_identity(nc, identity[:])
+        minus_one = held.tile([P, T], F32, name="minus_one")
+        nc.gpsimd.memset(minus_one[:], -1.0)
+        ones = held.tile([T, 1], F32, name="ones")
+        nc.gpsimd.memset(ones[:], 1.0)
+
+        shifted = [held.tile([P, N], F32, name=f"shifted{blk}") for blk in range(BLOCKS)]
+        w = [psum.tile([T, B], F32, name=f"w{i}") for i in range(K)]
         for i in reversed(range(K)):
-            rows = 2**i
-            picked = [
-                windows[blk][:].indirect(offsets[:, i * LIST_COLS : (i + 1) * LIST_COLS]) for blk in range(BLOCKS)
-            ]
-            if rows > 1:
-                folded = [held.tile([P, rows * T], F32, name=f"folded{i}_{blk}") for blk in range(BLOCKS)]
-            for m in reversed(range(rows)):
-                for blk in range(BLOCKS):
-                    if m > 0:
-                        product = folded[blk][:, m * T : (m + 1) * T]
-                    elif i > 0:
-                        product = early[blk][:, i * T : (i + 1) * T]
-                    else:
-                        product = late[:, blk * T : (blk + 1) * T]
-                    with_v = levels[blk][:, (2 * m + 1) * T : (2 * m + 2) * T]
-                    nc.vector.tensor_tensor(product, picked[blk], with_v, MULT)
-            if rows > 1:
-                for blk in range(BLOCKS):
-                    without_v = bit_halves(levels[blk][:], T)[0][:, 1:, :]
-                    products = folded[blk][:, T:].rearrange("p (m t) -> p m t", t=T)
-                    nc.vector.tensor_tensor(products, products, without_v, ADD)
-                levels = folded
+            for blk in range(BLOCKS):
+                picked = windows[blk][:].indirect(offsets[:, i * LIST_COLS : (i + 1) * LIST_COLS])
+                piece = shifted[blk][:, i * T : (i + 1) * T]
+                nc.vector.tensor_tensor(piece, picked, minus_one[:], ADD)
+                nc.tensor.transpose(w[i][:, blk * P : (blk + 1) * P], piece, identity[:])
 
-        early_sums = held.tile([P, BLOCKS], F32, name="early_sums")
-        unused = held.tile([P, K * T], F32, name="unused")
+        high_w1 = held.tile([T, B], F32, name="high_w1")
+        nc.scalar.activation(high_w1[:], w[2][:], IDENTITY, bias=d(6), scale=d(7))
+        low_w1 = held.tile([T, B], F32, name="low_w1")
+        nc.scalar.activation(low_w1[:], w[2][:], IDENTITY, bias=d(2), scale=d(3))
+
+        high = held.tile([T, B], F32, name="high")
+        nc.vector.tensor_tensor(high[:], w[1][:], high_w1[:], MULT)
+        low = held.tile([T, B], F32, name="low")
+        nc.vector.tensor_tensor(low[:], w[1][:], low_w1[:], MULT)
+        high_sum = held.tile([T, B], F32, name="high_sum")
+        nc.vector.scalar_tensor_tensor(high_sum[:], w[2][:], d(5), high[:], MULT, ADD)
+        low_sum = held.tile([T, B], F32, name="low_sum")
+        nc.vector.scalar_tensor_tensor(low_sum[:], w[2][:], d(1), low[:], MULT, ADD)
+        with_w0 = held.tile([T, B], F32, name="with_w0")
+        nc.vector.scalar_tensor_tensor(with_w0[:], high_sum[:], d(4), w[0][:], ADD, MULT)
+
+        f = held.tile([T, B], F32, name="f")
+        total_psum = psum.tile([1, B], F32, name="total_psum")
+        total = held.tile([1, B], F32, name="total")
         for blk in range(BLOCKS):
-            nc.scalar.activation(unused[:], early[blk][:], COPY, accum_out=early_sums[:, blk : blk + 1])
-        late_sums = held.tile([P, BLOCKS], F32, name="late_sums")
-        nc.vector.tensor_reduce(
-            late_sums[:], late[:].rearrange("p (n t) -> p n t", t=T), mybir.AxisListType.X, ADD
-        )
-
-        sums = held.tile([P, SQUARE], F32, name="sums", align_bytes=64)
-        nc.gpsimd.memset(sums[:], 0.0)
-        nc.vector.tensor_tensor(sums[:, 0:BLOCKS], late_sums[:], early_sums[:], ADD)
-
-        sums_t = held.tile([P, SQUARE], F32, name="sums_t", align_bytes=64)
-        nc.vector.transpose(sums_t[:], sums[:])
-        runs = sums_t[:].rearrange("(q j) i -> j q i", j=SQUARE)
-        for blk, queue in zip(range(BLOCKS), (nc.sync, nc.scalar)):
-            queue.dma_start(out[blk * P : (blk + 1) * P, :].rearrange("(q i) o -> q (i o)", i=SQUARE), runs[blk])
+            cols = slice(blk * P, (blk + 1) * P)
+            nc.vector.scalar_tensor_tensor(f[:, cols], low_sum[:, cols], d(0), with_w0[:, cols], ADD, ADD)
+            nc.tensor.matmul(total_psum[:, cols], ones[:], f[:, cols], start=True, stop=True)
+        nc.vector.tensor_copy(total[:], total_psum[:])
+        nc.sync.dma_start(out.rearrange("(o b) one -> o (b one)", o=1), total[:])

@@ -49,17 +49,17 @@ def tile_binarybnmodel_kernel(tc, x, cpds, offs, out):
         coef_psum = psum.tile([T, E], F32, name="coef_psum")
         nc.tensor.matmul(coef_psum[:], entries[:], weights[:], start=True, stop=True)
         coef = held.tile([T, E], F32, name="coef")
-        nc.scalar.activation(coef[:], coef_psum[:], IDENTITY)
+        nc.vector.tensor_copy(coef[:], coef_psum[:])
 
         def d(s):
             return coef[:, s : s + 1]
 
         identity = held.tile([P, P], F32, name="identity")
         make_identity(nc, identity[:])
-        minus_one = held.tile([P, T], F32, name="minus_one")
-        nc.gpsimd.memset(minus_one[:], -1.0)
-        ones = held.tile([T, 1], F32, name="ones")
+        ones = held.tile([P, T], F32, name="ones")
         nc.gpsimd.memset(ones[:], 1.0)
+        minus_one = held.tile([P, T], F32, name="minus_one")
+        nc.scalar.activation(minus_one[:], ones[:], IDENTITY, scale=-1.0)
 
         shifted = [held.tile([P, N], F32, name=f"shifted{blk}") for blk in range(BLOCKS)]
         w = [psum.tile([T, B], F32, name=f"w{i}") for i in range(K)]
@@ -92,6 +92,6 @@ def tile_binarybnmodel_kernel(tc, x, cpds, offs, out):
         for blk in range(BLOCKS):
             cols = slice(blk * P, (blk + 1) * P)
             nc.vector.scalar_tensor_tensor(f[:, cols], low_sum[:, cols], d(0), with_w0[:, cols], ADD, ADD)
-            nc.tensor.matmul(total_psum[:, cols], ones[:], f[:, cols], start=True, stop=True)
+            nc.tensor.matmul(total_psum[:, cols], ones[:, 0:1], f[:, cols], start=True, stop=True)
         nc.vector.tensor_copy(total[:], total_psum[:])
         nc.sync.dma_start(out.rearrange("(o b) one -> o (b one)", o=1), total[:])

@@ -14,6 +14,8 @@ T, K, E = 128, 3, 8
 N = K * T
 BLOCKS = B // P
 LIST_COLS = T // 16
+BRACKETS = E // 2
+SQUARE = 32
 
 
 def bit_halves(rows, low):
@@ -41,8 +43,8 @@ def tile_binarybnmodel_kernel(tc, x, cpds, offs, out):
 
         weights = held.tile([E, E], F32, name="weights")
         make_identity(nc, weights[:])
-        for low in (1, 2, 4):
-            bit_clear, bit_set = bit_halves(weights[:], low)
+        for bit_weight in (1, 2, 4):
+            bit_clear, bit_set = bit_halves(weights[:], bit_weight)
             nc.vector.tensor_tensor(bit_set, bit_set, bit_clear, SUBTRACT)
             nc.vector.tensor_tensor(bit_clear, bit_clear, bit_set, ADD)
 
@@ -51,9 +53,6 @@ def tile_binarybnmodel_kernel(tc, x, cpds, offs, out):
         coef = held.tile([T, E], F32, name="coef")
         nc.vector.tensor_copy(coef[:], coef_psum[:])
 
-        def d(s):
-            return coef[:, s : s + 1]
-
         identity = held.tile([P, P], F32, name="identity")
         make_identity(nc, identity[:])
         ones = held.tile([P, T], F32, name="ones")
@@ -61,37 +60,50 @@ def tile_binarybnmodel_kernel(tc, x, cpds, offs, out):
         minus_one = held.tile([P, T], F32, name="minus_one")
         nc.scalar.activation(minus_one[:], ones[:], IDENTITY, scale=-1.0)
 
-        shifted = [held.tile([P, N], F32, name=f"shifted{blk}") for blk in range(BLOCKS)]
-        w = [psum.tile([T, B], F32, name=f"w{i}") for i in range(K)]
+        w = [held.tile([P, BLOCKS, T], F32, name=f"w{i}") for i in range(K)]
         for i in reversed(range(K)):
             for blk in range(BLOCKS):
                 picked = windows[blk][:].indirect(offsets[:, i * LIST_COLS : (i + 1) * LIST_COLS])
-                piece = shifted[blk][:, i * T : (i + 1) * T]
-                nc.vector.tensor_tensor(piece, picked, minus_one[:], ADD)
-                nc.tensor.transpose(w[i][:, blk * P : (blk + 1) * P], piece, identity[:])
+                nc.vector.tensor_tensor(w[i][:, blk, :], picked, minus_one[:], ADD)
 
-        high_w1 = held.tile([T, B], F32, name="high_w1")
-        nc.scalar.activation(high_w1[:], w[2][:], IDENTITY, bias=d(6), scale=d(7))
-        low_w1 = held.tile([T, B], F32, name="low_w1")
-        nc.scalar.activation(low_w1[:], w[2][:], IDENTITY, bias=d(2), scale=d(3))
-
-        high = held.tile([T, B], F32, name="high")
-        nc.vector.tensor_tensor(high[:], w[1][:], high_w1[:], MULT)
-        low = held.tile([T, B], F32, name="low")
-        nc.vector.tensor_tensor(low[:], w[1][:], low_w1[:], MULT)
-        high_sum = held.tile([T, B], F32, name="high_sum")
-        nc.vector.scalar_tensor_tensor(high_sum[:], w[2][:], d(5), high[:], MULT, ADD)
-        low_sum = held.tile([T, B], F32, name="low_sum")
-        nc.vector.scalar_tensor_tensor(low_sum[:], w[2][:], d(1), low[:], MULT, ADD)
-        with_w0 = held.tile([T, B], F32, name="with_w0")
-        nc.vector.scalar_tensor_tensor(with_w0[:], high_sum[:], d(4), w[0][:], ADD, MULT)
-
-        f = held.tile([T, B], F32, name="f")
-        total_psum = psum.tile([1, B], F32, name="total_psum")
-        total = held.tile([1, B], F32, name="total")
+        w2_by_table = psum.tile([T, BLOCKS, P], F32, name="w2_by_table")
         for blk in range(BLOCKS):
-            cols = slice(blk * P, (blk + 1) * P)
-            nc.vector.scalar_tensor_tensor(f[:, cols], low_sum[:, cols], d(0), with_w0[:, cols], ADD, ADD)
-            nc.tensor.matmul(total_psum[:, cols], ones[:, 0:1], f[:, cols], start=True, stop=True)
-        nc.vector.tensor_copy(total[:], total_psum[:])
-        nc.sync.dma_start(out.rearrange("(o b) one -> o (b one)", o=1), total[:])
+            nc.tensor.transpose(w2_by_table[:, blk, :], w[2][:, blk, :], identity[:])
+
+        brackets = [None] * BRACKETS
+        for m in reversed(range(BRACKETS)):
+            by_table = held.tile([T, BLOCKS, P], F32, name=f"by_table{m}")
+            nc.scalar.activation(
+                by_table[:], w2_by_table[:], IDENTITY, bias=coef[:, 2 * m : 2 * m + 1], scale=coef[:, 2 * m + 1 : 2 * m + 2]
+            )
+            brackets[m] = psum.tile([P, BLOCKS, T], F32, name=f"bracket{m}")
+            for blk in range(BLOCKS):
+                nc.tensor.transpose(brackets[m][:, blk, :], by_table[:, blk, :], identity[:])
+
+        w0_w1 = held.tile([P, BLOCKS, T], F32, name="w0_w1")
+        nc.vector.tensor_tensor(w0_w1[:], w[0][:], w[1][:], MULT)
+        factors = [None, w[1], w[0], w0_w1]
+
+        partial = held.tile([P, BLOCKS, BRACKETS], F32, name="partial")
+        products = held.tile([P, BLOCKS, BRACKETS, T], F32, name="products")
+        for m in reversed(range(BRACKETS)):
+            for blk in range(BLOCKS):
+                if m > 0:
+                    nc.vector.scalar_tensor_tensor(
+                        products[:, blk, m, :], brackets[m][:, blk, :], 1.0, factors[m][:, blk, :], MULT, MULT,
+                        accum_out=partial[:, blk, m : m + 1],
+                    )
+                else:
+                    nc.scalar.activation(
+                        products[:, blk, m, :], brackets[m][:, blk, :], IDENTITY, accum_out=partial[:, blk, m : m + 1]
+                    )
+
+        sums = held.tile([P, SQUARE], F32, name="sums", align_bytes=64)
+        nc.gpsimd.memset(sums[:], 0.0)
+        nc.vector.tensor_reduce(sums[:, 0:BLOCKS], partial[:], mybir.AxisListType.X, ADD)
+
+        sums_t = held.tile([P, SQUARE], F32, name="sums_t", align_bytes=64)
+        nc.vector.transpose(sums_t[:], sums[:])
+        runs = sums_t[:].rearrange("(q j) i -> j q i", j=SQUARE)
+        for blk, queue in zip(range(BLOCKS), (nc.sync, nc.scalar)):
+            queue.dma_start(out[blk * P : (blk + 1) * P, :].rearrange("(q i) o -> q (i o)", i=SQUARE), runs[blk])

@@ -15,6 +15,7 @@ N = K * T
 BLOCKS = B // P
 LIST_COLS = T // 16
 BRACKETS = E // 2
+BRACKET_ORDER = (1, 2, 3, 0)
 SQUARE = 32
 
 
@@ -66,27 +67,28 @@ def tile_binarybnmodel_kernel(tc, x, cpds, offs, out):
                 picked = windows[blk][:].indirect(offsets[:, i * LIST_COLS : (i + 1) * LIST_COLS])
                 nc.vector.tensor_tensor(w[i][:, blk, :], picked, minus_one[:], ADD)
 
-        w2_by_table = psum.tile([T, BLOCKS, P], F32, name="w2_by_table")
+        w2_by_table = [psum.tile([T, P], F32, name=f"w2_by_table{blk}") for blk in range(BLOCKS)]
         for blk in range(BLOCKS):
-            nc.tensor.transpose(w2_by_table[:, blk, :], w[2][:, blk, :], identity[:])
+            nc.tensor.transpose(w2_by_table[blk][:], w[2][:, blk, :], identity[:])
 
         brackets = [None] * BRACKETS
-        for m in reversed(range(BRACKETS)):
+        for m in BRACKET_ORDER:
             by_table = held.tile([T, BLOCKS, P], F32, name=f"by_table{m}")
-            nc.scalar.activation(
-                by_table[:], w2_by_table[:], IDENTITY, bias=coef[:, 2 * m : 2 * m + 1], scale=coef[:, 2 * m + 1 : 2 * m + 2]
-            )
             brackets[m] = psum.tile([P, BLOCKS, T], F32, name=f"bracket{m}")
             for blk in range(BLOCKS):
+                nc.scalar.activation(
+                    by_table[:, blk, :], w2_by_table[blk][:], IDENTITY,
+                    bias=coef[:, 2 * m : 2 * m + 1], scale=coef[:, 2 * m + 1 : 2 * m + 2],
+                )
                 nc.tensor.transpose(brackets[m][:, blk, :], by_table[:, blk, :], identity[:])
 
         w0_w1 = held.tile([P, BLOCKS, T], F32, name="w0_w1")
-        nc.vector.tensor_tensor(w0_w1[:], w[0][:], w[1][:], MULT)
+        nc.gpsimd.tensor_tensor(w0_w1[:], w[0][:], w[1][:], MULT)
         factors = [None, w[1], w[0], w0_w1]
 
         partial = held.tile([P, BLOCKS, BRACKETS], F32, name="partial")
         products = held.tile([P, BLOCKS, BRACKETS, T], F32, name="products")
-        for m in reversed(range(BRACKETS)):
+        for m in BRACKET_ORDER:
             for blk in range(BLOCKS):
                 if m > 0:
                     nc.vector.scalar_tensor_tensor(

@@ -56,16 +56,19 @@ def tile_binarybnmodel_kernel(tc, x, cpds, offs, out):
 
         identity = held.tile([P, P], F32, name="identity")
         make_identity(nc, identity[:])
-        ones = held.tile([P, T], F32, name="ones")
+        ones = held.tile([P, 2 * T], F32, name="ones")
         nc.gpsimd.memset(ones[:], 1.0)
-        minus_one = held.tile([P, T], F32, name="minus_one")
+        minus_one = held.tile([P, 2 * T], F32, name="minus_one")
         nc.scalar.activation(minus_one[:], ones[:], IDENTITY, scale=-1.0)
 
-        w = [held.tile([P, BLOCKS, T], F32, name=f"w{i}") for i in range(K)]
-        for i in reversed(range(K)):
+        shifted = held.tile([P, BLOCKS, N], F32, name="shifted")
+        for first, last in ((2, 2), (0, 1)):
             for blk in range(BLOCKS):
-                picked = windows[blk][:].indirect(offsets[:, i * LIST_COLS : (i + 1) * LIST_COLS])
-                nc.vector.tensor_tensor(w[i][:, blk, :], picked, minus_one[:], ADD)
+                picked = windows[blk][:].indirect(offsets[:, first * LIST_COLS : (last + 1) * LIST_COLS])
+                nc.vector.tensor_tensor(
+                    shifted[:, blk, first * T : (last + 1) * T], picked, minus_one[:, 0 : (last + 1 - first) * T], ADD
+                )
+        w = [shifted[:, :, i * T : (i + 1) * T] for i in range(K)]
 
         w2_by_table = [psum.tile([T, P], F32, name=f"w2_by_table{blk}") for blk in range(BLOCKS)]
         for blk in range(BLOCKS):
@@ -83,8 +86,8 @@ def tile_binarybnmodel_kernel(tc, x, cpds, offs, out):
                 nc.tensor.transpose(brackets[m][:, blk, :], by_table[:, blk, :], identity[:])
 
         w0_w1 = held.tile([P, BLOCKS, T], F32, name="w0_w1")
-        nc.gpsimd.tensor_tensor(w0_w1[:], w[0][:], w[1][:], MULT)
-        factors = [None, w[1], w[0], w0_w1]
+        nc.gpsimd.tensor_tensor(w0_w1[:], w[0], w[1], MULT)
+        factors = [None, w[1], w[0], w0_w1[:]]
 
         partial = held.tile([P, BLOCKS, BRACKETS], F32, name="partial")
         products = held.tile([P, BLOCKS, BRACKETS, T], F32, name="products")

@@ -33,31 +33,27 @@ def tile_binarybnmodel_kernel(tc, x, cpds, offs, out):
         offsets = held.tile([P, N // 16], U16, name="offsets")
         nc.sync.dma_start(offsets[:], offs)
 
-        entries = held.tile([E, T], F32, name="entries")
-        nc.scalar.dma_start(entries[:], cpds)
-
         windows = []
         for blk in range(BLOCKS):
             window = held.tile([P, S], F32, name=f"window{blk}")
             nc.sync.dma_start(window[:], x[blk * P : (blk + 1) * P, :])
             windows.append(window)
 
-        weights = held.tile([E, E], F32, name="weights")
-        make_identity(nc, weights[:])
-        for bit_weight in (1, 2, 4):
-            bit_clear, bit_set = bit_halves(weights[:], bit_weight)
-            nc.vector.tensor_tensor(bit_set, bit_set, bit_clear, SUBTRACT)
-            nc.vector.tensor_tensor(bit_clear, bit_clear, bit_set, ADD)
-
-        coef_psum = psum.tile([T, E], F32, name="coef_psum")
-        nc.tensor.matmul(coef_psum[:], entries[:], weights[:], start=True, stop=True)
         coef = held.tile([T, E], F32, name="coef")
-        nc.vector.tensor_copy(coef[:], coef_psum[:])
+        with nc.allow_non_contiguous_dma(reason="8 values to a partition, 4 KiB in all"):
+            nc.sync.dma_start(coef[:], cpds.rearrange("e t -> t e"))
+
+        for bit_weight in (1, 2, 4):
+            bit_clear, bit_set = bit_halves(coef[:], bit_weight)
+            nc.gpsimd.tensor_tensor(bit_clear, bit_set, bit_clear, SUBTRACT)
+
+        def d(s):
+            return coef[:, E - 1 - s : E - s]
 
         identity = held.tile([P, P], F32, name="identity")
         make_identity(nc, identity[:])
         ones = held.tile([P, 2 * T], F32, name="ones")
-        nc.gpsimd.memset(ones[:], 1.0)
+        nc.vector.memset(ones[:], 1.0)
         minus_one = held.tile([P, 2 * T], F32, name="minus_one")
         nc.scalar.activation(minus_one[:], ones[:], IDENTITY, scale=-1.0)
 
@@ -81,12 +77,12 @@ def tile_binarybnmodel_kernel(tc, x, cpds, offs, out):
             for blk in range(BLOCKS):
                 nc.scalar.activation(
                     by_table[:, blk, :], w2_by_table[blk][:], IDENTITY,
-                    bias=coef[:, 2 * m : 2 * m + 1], scale=coef[:, 2 * m + 1 : 2 * m + 2],
+                    bias=d(2 * m), scale=d(2 * m + 1),
                 )
                 nc.tensor.transpose(brackets[m][:, blk, :], by_table[:, blk, :], identity[:])
 
         w0_w1 = held.tile([P, BLOCKS, T], F32, name="w0_w1")
-        nc.gpsimd.tensor_tensor(w0_w1[:], w[0], w[1], MULT)
+        nc.vector.tensor_tensor(w0_w1[:], w[0], w[1], MULT)
         factors = [None, w[1], w[0], w0_w1[:]]
 
         partial = held.tile([P, BLOCKS, BRACKETS], F32, name="partial")

@@ -15,7 +15,6 @@ N = K * T
 BLOCKS = B // P
 LIST_COLS = T // 16
 BRACKETS = E // 2
-BRACKET_ORDER = (1, 2, 3, 0)
 SQUARE = 32
 
 
@@ -57,51 +56,42 @@ def tile_binarybnmodel_kernel(tc, x, cpds, offs, out):
         minus_one = held.tile([P, 2 * T], F32, name="minus_one")
         nc.scalar.activation(minus_one[:], ones[:], IDENTITY, scale=-1.0)
 
-        shifted = held.tile([P, BLOCKS, N], F32, name="shifted")
-        for first, last in ((2, 2), (0, 1)):
-            for blk in range(BLOCKS):
-                picked = windows[blk][:].indirect(offsets[:, first * LIST_COLS : (last + 1) * LIST_COLS])
-                nc.vector.tensor_tensor(
-                    shifted[:, blk, first * T : (last + 1) * T], picked, minus_one[:, 0 : (last + 1 - first) * T], ADD
-                )
-        w = [shifted[:, :, i * T : (i + 1) * T] for i in range(K)]
+        factors = held.tile([P, BLOCKS, BRACKETS, T], F32, name="factors")
+        nc.vector.memset(factors[:, :, 0, :], 1.0)
+
+        w2 = held.tile([P, BLOCKS, T], F32, name="w2")
+        for blk in range(BLOCKS):
+            picked = windows[blk][:].indirect(offsets[:, 2 * LIST_COLS : 3 * LIST_COLS])
+            nc.vector.tensor_tensor(w2[:, blk, :], picked, minus_one[:, 0:T], ADD)
+        for blk in range(BLOCKS):
+            picked = windows[blk][:].indirect(offsets[:, 0 : 2 * LIST_COLS])
+            nc.vector.tensor_tensor(factors[:, blk, 1:3, :].rearrange("p j t -> p (j t)"), picked, minus_one[:], ADD)
+        nc.vector.tensor_tensor(factors[:, :, 3, :], factors[:, :, 1, :], factors[:, :, 2, :], MULT)
 
         w2_by_table = [psum.tile([T, P], F32, name=f"w2_by_table{blk}") for blk in range(BLOCKS)]
         for blk in range(BLOCKS):
-            nc.tensor.transpose(w2_by_table[blk][:], w[2][:, blk, :], identity[:])
-
-        brackets = [None] * BRACKETS
-        for m in BRACKET_ORDER:
-            by_table = held.tile([T, BLOCKS, P], F32, name=f"by_table{m}")
-            brackets[m] = psum.tile([P, BLOCKS, T], F32, name=f"bracket{m}")
-            for blk in range(BLOCKS):
-                nc.scalar.activation(
-                    by_table[:, blk, :], w2_by_table[blk][:], IDENTITY,
-                    bias=d(2 * m), scale=d(2 * m + 1),
-                )
-                nc.tensor.transpose(brackets[m][:, blk, :], by_table[:, blk, :], identity[:])
-
-        w0_w1 = held.tile([P, BLOCKS, T], F32, name="w0_w1")
-        nc.vector.tensor_tensor(w0_w1[:], w[0], w[1], MULT)
-        factors = [None, w[1], w[0], w0_w1[:]]
-
-        partial = held.tile([P, BLOCKS, BRACKETS], F32, name="partial")
-        products = held.tile([P, BLOCKS, BRACKETS, T], F32, name="products")
-        for m in BRACKET_ORDER:
-            for blk in range(BLOCKS):
-                if m > 0:
-                    nc.vector.scalar_tensor_tensor(
-                        products[:, blk, m, :], brackets[m][:, blk, :], 1.0, factors[m][:, blk, :], MULT, MULT,
-                        accum_out=partial[:, blk, m : m + 1],
-                    )
-                else:
-                    nc.scalar.activation(
-                        products[:, blk, m, :], brackets[m][:, blk, :], IDENTITY, accum_out=partial[:, blk, m : m + 1]
-                    )
+            nc.tensor.transpose(w2_by_table[blk][:], w2[:, blk, :], identity[:])
 
         sums = held.tile([P, SQUARE], F32, name="sums", align_bytes=64)
         nc.gpsimd.memset(sums[:], 0.0)
-        nc.vector.tensor_reduce(sums[:, 0:BLOCKS], partial[:], mybir.AxisListType.X, ADD)
+
+        products = held.tile([P, BLOCKS, BRACKETS * T], F32, name="products")
+        for blk in range(BLOCKS):
+            brackets = psum.tile([P, BRACKETS, T], F32, name=f"brackets{blk}")
+            for j in range(BRACKETS):
+                s = 4 * (j % 2) + 2 * (j // 2)
+                by_table = held.tile([T, P], F32, name=f"by_table{blk}_{j}")
+                nc.scalar.activation(by_table[:], w2_by_table[blk][:], IDENTITY, bias=d(s), scale=d(s + 1))
+                nc.tensor.transpose(brackets[:, j, :], by_table[:], identity[:])
+            nc.vector.scalar_tensor_tensor(
+                products[:, blk, :],
+                brackets[:].rearrange("p j t -> p (j t)"),
+                1.0,
+                factors[:, blk, :, :].rearrange("p j t -> p (j t)"),
+                MULT,
+                MULT,
+                accum_out=sums[:, blk : blk + 1],
+            )
 
         sums_t = held.tile([P, SQUARE], F32, name="sums_t", align_bytes=64)
         nc.vector.transpose(sums_t[:], sums[:])

@@ -32,17 +32,14 @@ def tile_binarybnmodel_kernel(tc, x, cpds, offs, out):
         offsets = held.tile([P, N // 16], U16, name="offsets")
         nc.sync.dma_start(offsets[:], offs)
 
-        windows = []
-        for blk in range(BLOCKS):
-            window = held.tile([P, S], F32, name=f"window{blk}")
-            nc.sync.dma_start(window[:], x[blk * P : (blk + 1) * P, :])
-            windows.append(window)
-
+        windows = [held.tile([P, S], F32, name=f"window{blk}") for blk in range(BLOCKS)]
         coef = held.tile([T, E], F32, name="coef")
+        nc.sync.dma_start(windows[0][:], x[0:P, :])
         with nc.allow_non_contiguous_dma(reason="8 values to a partition, 4 KiB in all"):
             nc.sync.dma_start(coef[:], cpds.rearrange("e t -> t e"))
+        nc.sync.dma_start(windows[1][:], x[P:B, :])
 
-        for bit_weight in (1, 2, 4):
+        for bit_weight in (1, 4, 2):
             bit_clear, bit_set = bit_halves(coef[:], bit_weight)
             nc.gpsimd.tensor_tensor(bit_clear, bit_set, bit_clear, SUBTRACT)
 
@@ -63,7 +60,6 @@ def tile_binarybnmodel_kernel(tc, x, cpds, offs, out):
         for blk in range(BLOCKS):
             picked = windows[blk][:].indirect(offsets[:, 2 * LIST_COLS : 3 * LIST_COLS])
             nc.vector.tensor_tensor(w2[:, blk, :], picked, minus_one[:, 0:T], ADD)
-        for blk in range(BLOCKS):
             picked = windows[blk][:].indirect(offsets[:, 0 : 2 * LIST_COLS])
             nc.vector.tensor_tensor(factors[:, blk, 1:3, :].rearrange("p j t -> p (j t)"), picked, minus_one[:], ADD)
         nc.vector.tensor_tensor(factors[:, :, 3, :], factors[:, :, 1, :], factors[:, :, 2, :], MULT)

@@ -41,7 +41,7 @@ def tile_binarybnmodel_kernel(tc, x, cpds, offs, out):
 
         for bit_weight in (1, 4, 2):
             bit_clear, bit_set = bit_halves(coef[:], bit_weight)
-            nc.gpsimd.tensor_tensor(bit_clear, bit_set, bit_clear, SUBTRACT)
+            nc.vector.tensor_tensor(bit_clear, bit_set, bit_clear, SUBTRACT)
 
         def d(s):
             return coef[:, E - 1 - s : E - s]

@@ -5,7 +5,6 @@ F32 = mybir.dt.float32
 U16 = mybir.dt.uint16
 MULT = mybir.AluOpType.mult
 ADD = mybir.AluOpType.add
-SUBTRACT = mybir.AluOpType.subtract
 IDENTITY = mybir.ActivationFunctionType.Identity
 
 P = 128
@@ -27,6 +26,7 @@ def tile_binarybnmodel_kernel(tc, x, cpds, offs, out):
     nc = tc.nc
     with (
         tc.tile_pool(name="held", bufs=1) as held,
+        tc.tile_pool(name="passing", bufs=1) as passing,
         tc.psum_pool(name="psum", bufs=1) as psum,
     ):
         offsets = held.tile([P, N // 16], U16, name="offsets")
@@ -34,14 +34,16 @@ def tile_binarybnmodel_kernel(tc, x, cpds, offs, out):
 
         windows = [held.tile([P, S], F32, name=f"window{blk}") for blk in range(BLOCKS)]
         coef = held.tile([T, E], F32, name="coef")
-        nc.sync.dma_start(windows[0][:], x[0:P, :])
+        for blk, queue in zip(range(BLOCKS), (nc.scalar, nc.sync)):
+            queue.dma_start(windows[blk][:], x[blk * P : (blk + 1) * P, :])
         with nc.allow_non_contiguous_dma(reason="8 values to a partition, 4 KiB in all"):
             nc.sync.dma_start(coef[:], cpds.rearrange("e t -> t e"))
-        nc.sync.dma_start(windows[1][:], x[P:B, :])
 
+        minus = passing.tile([P, 1], F32, name="minus")
+        nc.vector.memset(minus[:], -1.0)
         for bit_weight in (1, 4, 2):
             bit_clear, bit_set = bit_halves(coef[:], bit_weight)
-            nc.vector.tensor_tensor(bit_clear, bit_set, bit_clear, SUBTRACT)
+            nc.vector.scalar_tensor_tensor(bit_clear, bit_clear, minus[:], bit_set, MULT, ADD)
 
         def d(s):
             return coef[:, E - 1 - s : E - s]
@@ -53,16 +55,17 @@ def tile_binarybnmodel_kernel(tc, x, cpds, offs, out):
         minus_one = held.tile([P, 2 * T], F32, name="minus_one")
         nc.scalar.activation(minus_one[:], ones[:], IDENTITY, scale=-1.0)
 
-        factors = held.tile([P, BLOCKS, BRACKETS, T], F32, name="factors")
-        nc.vector.memset(factors[:, :, 0, :], 1.0)
-
         w2 = held.tile([P, BLOCKS, T], F32, name="w2")
         for blk in range(BLOCKS):
             picked = windows[blk][:].indirect(offsets[:, 2 * LIST_COLS : 3 * LIST_COLS])
             nc.vector.tensor_tensor(w2[:, blk, :], picked, minus_one[:, 0:T], ADD)
+
+        factors = passing.tile([P, BLOCKS, K * T + 1], F32, name="factors", tag="minus")
+        for blk in range(BLOCKS):
+            w0_w1 = factors[:, blk, 0 : 2 * T]
             picked = windows[blk][:].indirect(offsets[:, 0 : 2 * LIST_COLS])
-            nc.vector.tensor_tensor(factors[:, blk, 1:3, :].rearrange("p j t -> p (j t)"), picked, minus_one[:], ADD)
-        nc.vector.tensor_tensor(factors[:, :, 3, :], factors[:, :, 1, :], factors[:, :, 2, :], MULT)
+            nc.vector.tensor_tensor(w0_w1, picked, minus_one[:], ADD)
+            nc.vector.tensor_tensor(factors[:, blk, 2 * T : 3 * T], w0_w1[:, 0:T], w0_w1[:, T:], MULT)
 
         w2_by_table = [psum.tile([T, P], F32, name=f"w2_by_table{blk}") for blk in range(BLOCKS)]
         for blk in range(BLOCKS):
@@ -71,19 +74,24 @@ def tile_binarybnmodel_kernel(tc, x, cpds, offs, out):
         sums = held.tile([P, SQUARE], F32, name="sums", align_bytes=64)
         nc.gpsimd.memset(sums[:], 0.0)
 
-        products = held.tile([P, BLOCKS, BRACKETS * T], F32, name="products")
+        products = held.tile([P, BLOCKS, K * T + 1], F32, name="products")
+        unused = held.tile([P, BLOCKS, T], F32, name="unused")
         for blk in range(BLOCKS):
-            brackets = psum.tile([P, BRACKETS, T], F32, name=f"brackets{blk}")
+            bracket_0 = psum.tile([P, T], F32, name=f"bracket_0_{blk}")
+            brackets = psum.tile([P, BRACKETS * T], F32, name=f"brackets{blk}")
+            nc.tensor.transpose(brackets[:, K * T :], ones[:, 0:P], identity[:])
             for j in range(BRACKETS):
                 s = 4 * (j % 2) + 2 * (j // 2)
                 by_table = held.tile([T, P], F32, name=f"by_table{blk}_{j}")
                 nc.scalar.activation(by_table[:], w2_by_table[blk][:], IDENTITY, bias=d(s), scale=d(s + 1))
-                nc.tensor.transpose(brackets[:, j, :], by_table[:], identity[:])
+                turned = bracket_0[:] if j == 0 else brackets[:, (j - 1) * T : j * T]
+                nc.tensor.transpose(turned, by_table[:], identity[:])
+            nc.scalar.activation(unused[:, blk, :], bracket_0[:], IDENTITY, accum_out=factors[:, blk, K * T :])
             nc.vector.scalar_tensor_tensor(
                 products[:, blk, :],
-                brackets[:].rearrange("p j t -> p (j t)"),
+                brackets[:, 0 : K * T + 1],
                 1.0,
-                factors[:, blk, :, :].rearrange("p j t -> p (j t)"),
+                factors[:, blk, :],
                 MULT,
                 MULT,
                 accum_out=sums[:, blk : blk + 1],

@@ -34,10 +34,10 @@ def tile_binarybnmodel_kernel(tc, x, cpds, offs, out):
 
         windows = [held.tile([P, S], F32, name=f"window{blk}") for blk in range(BLOCKS)]
         coef = held.tile([T, E], F32, name="coef")
-        for blk, queue in zip(range(BLOCKS), (nc.scalar, nc.sync)):
-            queue.dma_start(windows[blk][:], x[blk * P : (blk + 1) * P, :])
+        nc.sync.dma_start(windows[0][:], x[0:P, :])
         with nc.allow_non_contiguous_dma(reason="8 values to a partition, 4 KiB in all"):
             nc.sync.dma_start(coef[:], cpds.rearrange("e t -> t e"))
+        nc.sync.dma_start(windows[1][:], x[P:B, :])
 
         minus = passing.tile([P, 1], F32, name="minus")
         nc.vector.memset(minus[:], -1.0)

@@ -50,10 +50,10 @@ def tile_binarybnmodel_kernel(tc, x, cpds, offs, out):
 
         identity = held.tile([P, P], F32, name="identity")
         make_identity(nc, identity[:])
-        ones = held.tile([P, 2 * T], F32, name="ones")
-        nc.vector.memset(ones[:], 1.0)
         minus_one = held.tile([P, 2 * T], F32, name="minus_one")
-        nc.scalar.activation(minus_one[:], ones[:], IDENTITY, scale=-1.0)
+        nc.vector.memset(minus_one[:], -1.0)
+        sums = held.tile([P, SQUARE], F32, name="sums", align_bytes=64)
+        nc.scalar.activation(sums[:], minus_one[:, 0:SQUARE], IDENTITY, scale=0.0)
 
         w2 = held.tile([P, BLOCKS, T], F32, name="w2")
         for blk in range(BLOCKS):
@@ -71,22 +71,19 @@ def tile_binarybnmodel_kernel(tc, x, cpds, offs, out):
         for blk in range(BLOCKS):
             nc.tensor.transpose(w2_by_table[blk][:], w2[:, blk, :], identity[:])
 
-        sums = held.tile([P, SQUARE], F32, name="sums", align_bytes=64)
-        nc.gpsimd.memset(sums[:], 0.0)
-
         products = held.tile([P, BLOCKS, K * T + 1], F32, name="products")
         unused = held.tile([P, BLOCKS, T], F32, name="unused")
         for blk in range(BLOCKS):
             bracket_0 = psum.tile([P, T], F32, name=f"bracket_0_{blk}")
             brackets = psum.tile([P, BRACKETS * T], F32, name=f"brackets{blk}")
-            nc.tensor.transpose(brackets[:, K * T :], ones[:, 0:P], identity[:])
+            nc.tensor.transpose(brackets[:, K * T :], minus_one[:, 0:P], identity[:])
             for j in range(BRACKETS):
                 s = 4 * (j % 2) + 2 * (j // 2)
                 by_table = held.tile([T, P], F32, name=f"by_table{blk}_{j}")
                 nc.scalar.activation(by_table[:], w2_by_table[blk][:], IDENTITY, bias=d(s), scale=d(s + 1))
                 turned = bracket_0[:] if j == 0 else brackets[:, (j - 1) * T : j * T]
                 nc.tensor.transpose(turned, by_table[:], identity[:])
-            nc.scalar.activation(unused[:, blk, :], bracket_0[:], IDENTITY, accum_out=factors[:, blk, K * T :])
+            nc.scalar.activation(unused[:, blk, :], bracket_0[:], IDENTITY, scale=-1.0, accum_out=factors[:, blk, K * T :])
             nc.vector.scalar_tensor_tensor(
                 products[:, blk, :],
                 brackets[:, 0 : K * T + 1],

import concourse.mybir as mybir
from concourse.masks import make_identity

F32 = mybir.dt.float32
U16 = mybir.dt.uint16
MULT = mybir.AluOpType.mult
ADD = mybir.AluOpType.add
IDENTITY = mybir.ActivationFunctionType.Identity

P = 128
B, S = 256, 256
T, K, E = 128, 3, 8
N = K * T
BLOCKS = B // P
LIST_COLS = T // 16
BRACKETS = E // 2
SQUARE = 32


def bit_halves(rows, low):
    view = rows.rearrange("p (h two l) -> p h two l", two=2, l=low)
    return view[:, :, 0, :], view[:, :, 1, :]


def tile_binarybnmodel_kernel(tc, x, cpds, offs, out):
    nc = tc.nc
    with (
        tc.tile_pool(name="held", bufs=1) as held,
        tc.tile_pool(name="passing", bufs=1) as passing,
        tc.psum_pool(name="psum", bufs=1) as psum,
    ):
        offsets = held.tile([P, N // 16], U16, name="offsets")
        nc.sync.dma_start(offsets[:], offs)

        windows = [held.tile([P, S], F32, name=f"window{blk}") for blk in range(BLOCKS)]
        coef = held.tile([T, E], F32, name="coef")
        nc.sync.dma_start(windows[0][:], x[0:P, :])
        with nc.allow_non_contiguous_dma(reason="8 values to a partition, 4 KiB in all"):
            nc.sync.dma_start(coef[:], cpds.rearrange("e t -> t e"))
        nc.sync.dma_start(windows[1][:], x[P:B, :])

        minus = passing.tile([P, 1], F32, name="minus")
        nc.vector.memset(minus[:], -1.0)
        for bit_weight in (1, 4, 2):
            bit_clear, bit_set = bit_halves(coef[:], bit_weight)
            nc.vector.scalar_tensor_tensor(bit_clear, bit_clear, minus[:], bit_set, MULT, ADD)

        def d(s):
            return coef[:, E - 1 - s : E - s]

        identity = held.tile([P, P], F32, name="identity")
        make_identity(nc, identity[:])
        minus_one = held.tile([P, 2 * T], F32, name="minus_one")
        nc.vector.memset(minus_one[:], -1.0)
        sums = held.tile([P, SQUARE], F32, name="sums", align_bytes=64)
        nc.scalar.activation(sums[:], minus_one[:, 0:SQUARE], IDENTITY, scale=0.0)

        w2 = held.tile([P, BLOCKS, T], F32, name="w2")
        for blk in range(BLOCKS):
            picked = windows[blk][:].indirect(offsets[:, 2 * LIST_COLS : 3 * LIST_COLS])
            nc.vector.tensor_tensor(w2[:, blk, :], picked, minus_one[:, 0:T], ADD)

        factors = passing.tile([P, BLOCKS, K * T + 1], F32, name="factors", tag="minus")
        for blk in range(BLOCKS):
            w0_w1 = factors[:, blk, 0 : 2 * T]
            picked = windows[blk][:].indirect(offsets[:, 0 : 2 * LIST_COLS])
            nc.vector.tensor_tensor(w0_w1, picked, minus_one[:], ADD)
            nc.vector.tensor_tensor(factors[:, blk, 2 * T : 3 * T], w0_w1[:, 0:T], w0_w1[:, T:], MULT)

        w2_by_table = [psum.tile([T, P], F32, name=f"w2_by_table{blk}") for blk in range(BLOCKS)]
        for blk in range(BLOCKS):
            nc.tensor.transpose(w2_by_table[blk][:], w2[:, blk, :], identity[:])

        products = held.tile([P, BLOCKS, K * T + 1], F32, name="products")
        unused = held.tile([P, BLOCKS, T], F32, name="unused")
        for blk in range(BLOCKS):
            bracket_0 = psum.tile([P, T], F32, name=f"bracket_0_{blk}")
            brackets = psum.tile([P, BRACKETS * T], F32, name=f"brackets{blk}")
            nc.tensor.transpose(brackets[:, K * T :], minus_one[:, 0:P], identity[:])
            for j in range(BRACKETS):
                s = 4 * (j % 2) + 2 * (j // 2)
                by_table = held.tile([T, P], F32, name=f"by_table{blk}_{j}")
                nc.scalar.activation(by_table[:], w2_by_table[blk][:], IDENTITY, bias=d(s), scale=d(s + 1))
                turned = bracket_0[:] if j == 0 else brackets[:, (j - 1) * T : j * T]
                nc.tensor.transpose(turned, by_table[:], identity[:])
            nc.scalar.activation(unused[:, blk, :], bracket_0[:], IDENTITY, scale=-1.0, accum_out=factors[:, blk, K * T :])
            nc.vector.scalar_tensor_tensor(
                products[:, blk, :],
                brackets[:, 0 : K * T + 1],
                1.0,
                factors[:, blk, :],
                MULT,
                MULT,
                accum_out=sums[:, blk : blk + 1],
            )

        sums_t = held.tile([P, SQUARE], F32, name="sums_t", align_bytes=64)
        nc.vector.transpose(sums_t[:], sums[:])
        runs = sums_t[:].rearrange("(q j) i -> j q i", j=SQUARE)
        for blk, queue in zip(range(BLOCKS), (nc.sync, nc.scalar)):
            queue.dma_start(out[blk * P : (blk + 1) * P, :].rearrange("(q i) o -> q (i o)", i=SQUARE), runs[blk])
